import numpy as np
import ml_dtypes

BF16 = ml_dtypes.bfloat16


def bf(x):
    return np.asarray(x, np.float32).astype(BF16)


def f32(x):
    return np.asarray(x, np.float32)


def f64(x):
    return np.asarray(x).astype(np.float64)


def striped(idx):
    return np.tile(idx.reshape(-1, 16).T, (8, 1))


V, S, E, R, N = 1024, 1024, 128, 8, 512


def setup_inputs():
    return {"rel": f32(np.random.choice(R + 1, size=(V, S))), "embed": bf(np.random.standard_normal((V, E))), "src_embed": bf(2.0 * np.random.standard_normal((E, N)) / np.sqrt(E)), "offs": striped(np.random.permutation(np.tile(np.arange(S), 2))[:N])}


def reference(rel, embed, src_embed, offs):
    idx = offs[:16].T.reshape(-1)
    picked = f64(rel)[:, idx]
    base = f64(embed) @ f64(src_embed)
    parts = []
    for r in range(R):
        p = np.exp((picked == r + 1) * base)
        parts.append((f64(embed).T @ p) / p.sum(axis=0, keepdims=True))
    return np.concatenate(parts, axis=0)

@@ -1,0 +1,73 @@
+import concourse.mybir as mybir
+from concourse.masks import make_identity
+
+V, S, E, R, N = 1024, 1024, 128, 8, 512
+P = 128
+VB = V // P
+FLOPS = 2 * V * E * N * (R + 1)
+
+F32 = mybir.dt.float32
+BF16 = mybir.dt.bfloat16
+U16 = mybir.dt.uint16
+ACT = mybir.ActivationFunctionType
+ALU = mybir.AluOpType
+
+
+def tile_graphattention_kernel(tc, rel, embed, src_embed, offs, out):
+    nc = tc.nc
+    with (
+        tc.tile_pool(name="held", bufs=1) as held,
+        tc.tile_pool(name="work", bufs=3) as work,
+        tc.psum_pool(name="setup_ps", bufs=1) as setup_ps,
+        tc.psum_pool(name="acc_ps", bufs=2) as acc_ps,
+    ):
+        offsets = held.tile([P, N // 16], U16, name="offsets")
+        nc.sync.dma_start(offsets[:], offs)
+        embed_sb = held.tile([P, VB, E], BF16, name="embed_sb")
+        nc.sync.dma_start(embed_sb[:], embed.rearrange("(b p) e -> p b e", p=P))
+        src_sb = held.tile([E, N], BF16, name="src_sb")
+        nc.sync.dma_start(src_sb[:], src_embed)
+        rel_sb = [held.tile([P, S], F32, name=f"rel{b}") for b in range(VB)]
+        for b in range(VB):
+            nc.sync.dma_start(rel_sb[b][:], rel[b * P : (b + 1) * P, :])
+
+        ident = held.tile([P, P], BF16, name="ident")
+        make_identity(nc, ident[:])
+        ones = held.tile([P, P], BF16, name="ones")
+        nc.gpsimd.memset(ones[:], 1.0)
+
+        embT_ps = setup_ps.tile([E, V], BF16, name="embT_ps")
+        for b in range(VB):
+            nc.tensor.transpose(embT_ps[:, b * P : (b + 1) * P], embed_sb[:, b, :], ident[:])
+        embT = held.tile([E, V], BF16, name="embT")
+        nc.vector.tensor_copy(embT[:], embT_ps[:])
+
+        base = []
+        picked = []
+        for b in range(VB):
+            base_ps = setup_ps.tile([P, N], F32, name="base_ps", bufs=2)
+            nc.tensor.matmul(base_ps[:], embT[:, b * P : (b + 1) * P], src_sb[:], start=True, stop=True)
+            base_b = held.tile([P, N], F32, name=f"base{b}")
+            nc.vector.tensor_copy(base_b[:], base_ps[:])
+            base.append(base_b)
+            picked_b = held.tile([P, N], F32, name=f"picked{b}")
+            nc.scalar.activation(picked_b[:], rel_sb[b][:].indirect(offsets[:]), ACT.Copy)
+            picked.append(picked_b)
+
+        for r in range(R):
+            num_ps = acc_ps.tile([E, N], F32, name="num_ps")
+            den_ps = acc_ps.tile([P, N], F32, name="den_ps")
+            for b in range(VB):
+                score = work.tile([P, N], F32, name="score")
+                nc.vector.scalar_tensor_tensor(
+                    score[:], picked[b][:], float(r + 1), base[b][:], ALU.is_equal, ALU.mult
+                )
+                prob = work.tile([P, N], BF16, name="prob")
+                nc.scalar.activation(prob[:], score[:], ACT.Exp)
+                nc.tensor.matmul(num_ps[:], embed_sb[:, b, :], prob[:], start=(b == 0), stop=(b == VB - 1))
+                nc.tensor.matmul(den_ps[:], ones[:], prob[:], start=(b == 0), stop=(b == VB - 1))
+            recip = work.tile([P, N], F32, name="recip")
+            nc.vector.reciprocal(recip[:], den_ps[:])
+            res = work.tile([E, N], F32, name="res")
+            nc.vector.tensor_tensor(res[:], num_ps[:], recip[:], ALU.mult)
+            nc.sync.dma_start(out[r * E : (r + 1) * E, :], res[:])

@@ -4,6 +4,10 @@ from concourse.masks import make_identity
 V, S, E, R, N = 1024, 1024, 128, 8, 512
 P = 128
 VB = V // P
+QUAD = 32
+NQ = P // QUAD
+AHEAD = 2
+LEAD = 2
 FLOPS = 2 * V * E * N * (R + 1)
 
 F32 = mybir.dt.float32
@@ -13,13 +17,18 @@ ACT = mybir.ActivationFunctionType
 ALU = mybir.AluOpType
 
 
+def quadrant(c):
+    return slice(c * QUAD, (c + 1) * QUAD)
+
+
 def tile_graphattention_kernel(tc, rel, embed, src_embed, offs, out):
     nc = tc.nc
     with (
         tc.tile_pool(name="held", bufs=1) as held,
+        tc.tile_pool(name="qpool", bufs=(LEAD + 2) * NQ) as qpool,
         tc.tile_pool(name="work", bufs=3) as work,
-        tc.psum_pool(name="setup_ps", bufs=1) as setup_ps,
-        tc.psum_pool(name="acc_ps", bufs=2) as acc_ps,
+        tc.psum_pool(name="setup_ps", bufs=AHEAD) as setup_ps,
+        tc.psum_pool(name="acc_ps", bufs=NQ + 2) as acc_ps,
     ):
         offsets = held.tile([P, N // 16], U16, name="offsets")
         nc.sync.dma_start(offsets[:], offs)
@@ -33,41 +42,87 @@ def tile_graphattention_kernel(tc, rel, embed, src_embed, offs, out):
 
         ident = held.tile([P, P], BF16, name="ident")
         make_identity(nc, ident[:])
-        ones = held.tile([P, P], BF16, name="ones")
+        ones = held.tile([P, QUAD], BF16, name="ones")
         nc.gpsimd.memset(ones[:], 1.0)
+        one_f32 = held.tile([P, 1], F32, name="one_f32")
+        nc.gpsimd.memset(one_f32[:], 1.0)
 
-        embT_ps = setup_ps.tile([E, V], BF16, name="embT_ps")
+        embT_ps = setup_ps.tile([E, V], BF16, name="embT_ps", tag="setup")
+        embT = held.tile([E, V], BF16, name="embT")
         for b in range(VB):
             nc.tensor.transpose(embT_ps[:, b * P : (b + 1) * P], embed_sb[:, b, :], ident[:])
-        embT = held.tile([E, V], BF16, name="embT")
-        nc.vector.tensor_copy(embT[:], embT_ps[:])
+            nc.vector.tensor_copy(embT[:, b * P : (b + 1) * P], embT_ps[:, b * P : (b + 1) * P])
 
-        base = []
-        picked = []
-        for b in range(VB):
-            base_ps = setup_ps.tile([P, N], F32, name="base_ps", bufs=2)
+        picked = [held.tile([P, N], F32, name=f"picked{b}") for b in range(VB)]
+        gain = [held.tile([P, N], F32, name=f"gain{b}") for b in range(VB)]
+
+        def prepare_block(b):
+            base_ps = setup_ps.tile([P, N], F32, name="base_ps", tag="setup")
             nc.tensor.matmul(base_ps[:], embT[:, b * P : (b + 1) * P], src_sb[:], start=True, stop=True)
-            base_b = held.tile([P, N], F32, name=f"base{b}")
-            nc.vector.tensor_copy(base_b[:], base_ps[:])
-            base.append(base_b)
-            picked_b = held.tile([P, N], F32, name=f"picked{b}")
-            nc.scalar.activation(picked_b[:], rel_sb[b][:].indirect(offsets[:]), ACT.Copy)
-            picked.append(picked_b)
+            expo = work.tile([P, N], F32, name="expo")
+            nc.scalar.activation(expo[:], base_ps[:], ACT.Exp)
+            nc.gpsimd.tensor_scalar(gain[b][:], expo[:], -1.0, 1.0, ALU.add, ALU.mult)
+            nc.scalar.activation(picked[b][:], rel_sb[b][:].indirect(offsets[:]), ACT.Copy)
 
-        for r in range(R):
-            num_ps = acc_ps.tile([E, N], F32, name="num_ps")
-            den_ps = acc_ps.tile([P, N], F32, name="den_ps")
-            for b in range(VB):
-                score = work.tile([P, N], F32, name="score")
-                nc.vector.scalar_tensor_tensor(
-                    score[:], picked[b][:], float(r + 1), base[b][:], ALU.is_equal, ALU.mult
+        for b in range(AHEAD):
+            prepare_block(b)
+
+        block_sum = held.tile([P, E], F32, name="block_sum")
+        nc.vector.reduce_sum(block_sum[:], embed_sb[:].rearrange("p b e -> p e b"), axis=mybir.AxisListType.X)
+        esum_ps = acc_ps.tile([P, N], F32, name="bank")
+        for a in range(NQ):
+            for c in range(NQ):
+                nc.tensor.matmul(
+                    esum_ps[quadrant(c), a : a + 1], block_sum[:, quadrant(a)], one_f32[:], start=True, stop=True
                 )
-                prob = work.tile([P, N], BF16, name="prob")
-                nc.scalar.activation(prob[:], score[:], ACT.Exp)
-                nc.tensor.matmul(num_ps[:], embed_sb[:, b, :], prob[:], start=(b == 0), stop=(b == VB - 1))
-                nc.tensor.matmul(den_ps[:], ones[:], prob[:], start=(b == 0), stop=(b == VB - 1))
+        embed_sum = held.tile([P, NQ], F32, name="embed_sum")
+        nc.vector.tensor_copy(embed_sum[:], esum_ps[:, 0:NQ])
+
+        def make_q(first, b):
+            q = [qpool.tile([P, N], BF16, name="q") for c in range(NQ)]
+            for c in range(NQ):
+                nc.vector.scalar_tensor_tensor(
+                    q[c][:], picked[b][:], float(first + c + 1), gain[b][:], ALU.is_equal, ALU.mult
+                )
+            return q
+
+        def accumulate(num_ps, den_ps, b, q):
+            for c in range(NQ):
+                nc.tensor.matmul(den_ps[quadrant(c), :], ones[:], q[c][:], start=(b == 0), stop=(b == VB - 1))
+            for a in range(NQ):
+                for c in range(NQ):
+                    nc.tensor.matmul(
+                        num_ps[a][quadrant(c), :], embed_sb[:, b, quadrant(a)], q[c][:],
+                        start=(b == 0), stop=(b == VB - 1),
+                    )
+
+        def finish(first, num_ps, den_ps):
+            rsqrt = work.tile([P, N], F32, name="rsqrt")
+            nc.scalar.activation(rsqrt[:], den_ps[:], ACT.Abs_reciprocal_sqrt, bias=float(V))
             recip = work.tile([P, N], F32, name="recip")
-            nc.vector.reciprocal(recip[:], den_ps[:])
-            res = work.tile([E, N], F32, name="res")
-            nc.vector.tensor_tensor(res[:], num_ps[:], recip[:], ALU.mult)
-            nc.sync.dma_start(out[r * E : (r + 1) * E, :], res[:])
+            nc.scalar.activation(recip[:], rsqrt[:], ACT.Square)
+            for a in range(NQ):
+                res = work.tile([P, N], F32, name="res")
+                nc.vector.scalar_tensor_tensor(
+                    res[:], num_ps[a][:], embed_sum[:, a : a + 1], recip[:], ALU.add, ALU.mult
+                )
+                for c in range(NQ):
+                    row = (first + c) * E + a * QUAD
+                    nc.sync.dma_start(out[row : row + QUAD, :], res[quadrant(c), :])
+
+        steps = [(first, b) for first in range(0, R, NQ) for b in range(VB)]
+        q_of = {}
+        for i in range(len(steps) + LEAD):
+            if i < len(steps):
+                first, b = steps[i]
+                if first == 0 and b + AHEAD < VB:
+                    prepare_block(b + AHEAD)
+                q_of[steps[i]] = make_q(first, b)
+            if i >= LEAD:
+                first, b = steps[i - LEAD]
+                if b == 0:
+                    den_ps = acc_ps.tile([P, N], F32, name="bank")
+                    num_ps = [acc_ps.tile([P, N], F32, name="bank") for a in range(NQ)]
+                accumulate(num_ps, den_ps, b, q_of.pop(steps[i - LEAD]))
+                if b == VB - 1:
+                    finish(first, num_ps, den_ps)

@@ -4,11 +4,10 @@ from concourse.masks import make_identity
 V, S, E, R, N = 1024, 1024, 128, 8, 512
 P = 128
 VB = V // P
-QUAD = 32
-NQ = P // QUAD
-AHEAD = 2
-LEAD = 2
 FLOPS = 2 * V * E * N * (R + 1)
+
+GROUPS = ((0, 1, 2), (3,), (4,), (5,), (6,), (7,))
+AHEAD = 2
 
 F32 = mybir.dt.float32
 BF16 = mybir.dt.bfloat16
@@ -17,18 +16,14 @@ ACT = mybir.ActivationFunctionType
 ALU = mybir.AluOpType
 
 
-def quadrant(c):
-    return slice(c * QUAD, (c + 1) * QUAD)
-
-
 def tile_graphattention_kernel(tc, rel, embed, src_embed, offs, out):
     nc = tc.nc
     with (
         tc.tile_pool(name="held", bufs=1) as held,
-        tc.tile_pool(name="qpool", bufs=(LEAD + 2) * NQ) as qpool,
+        tc.tile_pool(name="qpool", bufs=12) as qpool,
         tc.tile_pool(name="work", bufs=3) as work,
         tc.psum_pool(name="setup_ps", bufs=AHEAD) as setup_ps,
-        tc.psum_pool(name="acc_ps", bufs=NQ + 2) as acc_ps,
+        tc.psum_pool(name="acc_ps", bufs=6) as acc_ps,
     ):
         offsets = held.tile([P, N // 16], U16, name="offsets")
         nc.sync.dma_start(offsets[:], offs)
@@ -40,18 +35,22 @@ def tile_graphattention_kernel(tc, rel, embed, src_embed, offs, out):
         for b in range(VB):
             nc.sync.dma_start(rel_sb[b][:], rel[b * P : (b + 1) * P, :])
 
+        warm = held.tile([P, 2], F32, name="warm")
+        nc.vector.memset(warm[:, 0:1], 0.0)
+        nc.scalar.activation(warm[:, 1:2], warm[:, 0:1], ACT.Exp)
+
         ident = held.tile([P, P], BF16, name="ident")
         make_identity(nc, ident[:])
-        ones = held.tile([P, QUAD], BF16, name="ones")
+        ones = held.tile([P, P], BF16, name="ones")
         nc.gpsimd.memset(ones[:], 1.0)
-        one_f32 = held.tile([P, 1], F32, name="one_f32")
-        nc.gpsimd.memset(one_f32[:], 1.0)
 
         embT_ps = setup_ps.tile([E, V], BF16, name="embT_ps", tag="setup")
         embT = held.tile([E, V], BF16, name="embT")
         for b in range(VB):
             nc.tensor.transpose(embT_ps[:, b * P : (b + 1) * P], embed_sb[:, b, :], ident[:])
             nc.vector.tensor_copy(embT[:, b * P : (b + 1) * P], embT_ps[:, b * P : (b + 1) * P])
+        embed_sum = held.tile([E, 1], F32, name="embed_sum")
+        nc.vector.reduce_sum(embed_sum[:], embT[:], axis=mybir.AxisListType.X)
 
         picked = [held.tile([P, N], F32, name=f"picked{b}") for b in range(VB)]
         gain = [held.tile([P, N], F32, name=f"gain{b}") for b in range(VB)]
@@ -64,65 +63,31 @@ def tile_graphattention_kernel(tc, rel, embed, src_embed, offs, out):
             nc.gpsimd.tensor_scalar(gain[b][:], expo[:], -1.0, 1.0, ALU.add, ALU.mult)
             nc.scalar.activation(picked[b][:], rel_sb[b][:].indirect(offsets[:]), ACT.Copy)
 
-        for b in range(AHEAD):
-            prepare_block(b)
-
-        block_sum = held.tile([P, E], F32, name="block_sum")
-        nc.vector.reduce_sum(block_sum[:], embed_sb[:].rearrange("p b e -> p e b"), axis=mybir.AxisListType.X)
-        esum_ps = acc_ps.tile([P, N], F32, name="bank")
-        for a in range(NQ):
-            for c in range(NQ):
-                nc.tensor.matmul(
-                    esum_ps[quadrant(c), a : a + 1], block_sum[:, quadrant(a)], one_f32[:], start=True, stop=True
-                )
-        embed_sum = held.tile([P, NQ], F32, name="embed_sum")
-        nc.vector.tensor_copy(embed_sum[:], esum_ps[:, 0:NQ])
-
-        def make_q(first, b):
-            q = [qpool.tile([P, N], BF16, name="q") for c in range(NQ)]
-            for c in range(NQ):
-                nc.vector.scalar_tensor_tensor(
-                    q[c][:], picked[b][:], float(first + c + 1), gain[b][:], ALU.is_equal, ALU.mult
-                )
-            return q
-
-        def accumulate(num_ps, den_ps, b, q):
-            for c in range(NQ):
-                nc.tensor.matmul(den_ps[quadrant(c), :], ones[:], q[c][:], start=(b == 0), stop=(b == VB - 1))
-            for a in range(NQ):
-                for c in range(NQ):
-                    nc.tensor.matmul(
-                        num_ps[a][quadrant(c), :], embed_sb[:, b, quadrant(a)], q[c][:],
-                        start=(b == 0), stop=(b == VB - 1),
-                    )
-
-        def finish(first, num_ps, den_ps):
+        def finish(r, num_ps, den_ps):
             rsqrt = work.tile([P, N], F32, name="rsqrt")
             nc.scalar.activation(rsqrt[:], den_ps[:], ACT.Abs_reciprocal_sqrt, bias=float(V))
+            num = work.tile([E, N], F32, name="num")
+            nc.scalar.activation(num[:], num_ps[:], ACT.Identity, bias=embed_sum[:, 0:1])
             recip = work.tile([P, N], F32, name="recip")
             nc.scalar.activation(recip[:], rsqrt[:], ACT.Square)
-            for a in range(NQ):
-                res = work.tile([P, N], F32, name="res")
-                nc.vector.scalar_tensor_tensor(
-                    res[:], num_ps[a][:], embed_sum[:, a : a + 1], recip[:], ALU.add, ALU.mult
-                )
-                for c in range(NQ):
-                    row = (first + c) * E + a * QUAD
-                    nc.sync.dma_start(out[row : row + QUAD, :], res[quadrant(c), :])
+            res = work.tile([E, N], F32, name="res")
+            nc.gpsimd.tensor_tensor(res[:], num[:], recip[:], ALU.mult)
+            nc.sync.dma_start(out[r * E : (r + 1) * E, :], res[:])
 
-        steps = [(first, b) for first in range(0, R, NQ) for b in range(VB)]
-        q_of = {}
-        for i in range(len(steps) + LEAD):
-            if i < len(steps):
-                first, b = steps[i]
-                if first == 0 and b + AHEAD < VB:
+        for b in range(AHEAD):
+            prepare_block(b)
+        for group in GROUPS:
+            num_ps = {r: acc_ps.tile([E, N], F32, name="bank") for r in group}
+            den_ps = {r: acc_ps.tile([P, N], F32, name="bank") for r in group}
+            for b in range(VB):
+                if group == GROUPS[0] and b + AHEAD < VB:
                     prepare_block(b + AHEAD)
-                q_of[steps[i]] = make_q(first, b)
-            if i >= LEAD:
-                first, b = steps[i - LEAD]
-                if b == 0:
-                    den_ps = acc_ps.tile([P, N], F32, name="bank")
-                    num_ps = [acc_ps.tile([P, N], F32, name="bank") for a in range(NQ)]
-                accumulate(num_ps, den_ps, b, q_of.pop(steps[i - LEAD]))
-                if b == VB - 1:
-                    finish(first, num_ps, den_ps)
+                for r in group:
+                    q = qpool.tile([P, N], BF16, name="q")
+                    nc.vector.scalar_tensor_tensor(
+                        q[:], picked[b][:], float(r + 1), gain[b][:], ALU.is_equal, ALU.mult
+                    )
+                    nc.tensor.matmul(den_ps[r][:], ones[:], q[:], start=(b == 0), stop=(b == VB - 1))
+                    nc.tensor.matmul(num_ps[r][:], embed_sb[:, b, :], q[:], start=(b == 0), stop=(b == VB - 1))
+            for r in group:
+                finish(r, num_ps[r], den_ps[r])

@@ -35,8 +35,8 @@ def tile_graphattention_kernel(tc, rel, embed, src_embed, offs, out):
         for b in range(VB):
             nc.sync.dma_start(rel_sb[b][:], rel[b * P : (b + 1) * P, :])
 
-        warm = held.tile([P, 2], F32, name="warm")
-        nc.vector.memset(warm[:, 0:1], 0.0)
+        warm = held.tile([P, 3], F32, name="warm")
+        nc.vector.memset(warm[:, 0:1], 1.0)
         nc.scalar.activation(warm[:, 1:2], warm[:, 0:1], ACT.Exp)
 
         ident = held.tile([P, P], BF16, name="ident")
@@ -44,23 +44,26 @@ def tile_graphattention_kernel(tc, rel, embed, src_embed, offs, out):
         ones = held.tile([P, P], BF16, name="ones")
         nc.gpsimd.memset(ones[:], 1.0)
 
-        embT_ps = setup_ps.tile([E, V], BF16, name="embT_ps", tag="setup")
         embT = held.tile([E, V], BF16, name="embT")
-        for b in range(VB):
-            nc.tensor.transpose(embT_ps[:, b * P : (b + 1) * P], embed_sb[:, b, :], ident[:])
-            nc.vector.tensor_copy(embT[:, b * P : (b + 1) * P], embT_ps[:, b * P : (b + 1) * P])
+        for first in range(0, VB, 4):
+            embT_ps = setup_ps.tile([E, 4 * P], BF16, name="embT_ps", tag="setup")
+            for k in range(4):
+                nc.tensor.transpose(embT_ps[:, k * P : (k + 1) * P], embed_sb[:, first + k, :], ident[:])
+            nc.vector.tensor_copy(embT[:, first * P : (first + 4) * P], embT_ps[:])
         embed_sum = held.tile([E, 1], F32, name="embed_sum")
         nc.vector.reduce_sum(embed_sum[:], embT[:], axis=mybir.AxisListType.X)
 
-        picked = [held.tile([P, N], F32, name=f"picked{b}") for b in range(VB)]
-        gain = [held.tile([P, N], F32, name=f"gain{b}") for b in range(VB)]
+        picked = {}
+        gain = {}
 
         def prepare_block(b):
             base_ps = setup_ps.tile([P, N], F32, name="base_ps", tag="setup")
             nc.tensor.matmul(base_ps[:], embT[:, b * P : (b + 1) * P], src_sb[:], start=True, stop=True)
             expo = work.tile([P, N], F32, name="expo")
             nc.scalar.activation(expo[:], base_ps[:], ACT.Exp)
-            nc.gpsimd.tensor_scalar(gain[b][:], expo[:], -1.0, 1.0, ALU.add, ALU.mult)
+            gain[b] = held.tile([P, N], F32, name=f"gain{b}")
+            nc.vector.tensor_scalar_add(gain[b][:], expo[:], -1.0)
+            picked[b] = held.tile([P, N], F32, name=f"picked{b}")
             nc.scalar.activation(picked[b][:], rel_sb[b][:].indirect(offsets[:]), ACT.Copy)
 
         def finish(r, num_ps, den_ps):
@@ -71,17 +74,19 @@ def tile_graphattention_kernel(tc, rel, embed, src_embed, offs, out):
             recip = work.tile([P, N], F32, name="recip")
             nc.scalar.activation(recip[:], rsqrt[:], ACT.Square)
             res = work.tile([E, N], F32, name="res")
-            nc.gpsimd.tensor_tensor(res[:], num[:], recip[:], ALU.mult)
+            nc.vector.tensor_tensor(res[:], num[:], recip[:], ALU.mult)
             nc.sync.dma_start(out[r * E : (r + 1) * E, :], res[:])
 
         for b in range(AHEAD):
             prepare_block(b)
         for group in GROUPS:
-            num_ps = {r: acc_ps.tile([E, N], F32, name="bank") for r in group}
             den_ps = {r: acc_ps.tile([P, N], F32, name="bank") for r in group}
+            num_ps = {r: acc_ps.tile([E, N], F32, name="bank") for r in group}
             for b in range(VB):
                 if group == GROUPS[0] and b + AHEAD < VB:
                     prepare_block(b + AHEAD)
+                if group == GROUPS[0] and b + AHEAD == VB:
+                    nc.scalar.activation(warm[:, 2:3], warm[:, 0:1], ACT.Abs_reciprocal_sqrt)
                 for r in group:
                     q = qpool.tile([P, N], BF16, name="q")
                     nc.vector.scalar_tensor_tensor(

@@ -4,10 +4,11 @@ from concourse.masks import make_identity
 V, S, E, R, N = 1024, 1024, 128, 8, 512
 P = 128
 VB = V // P
+BANKS = 8
 FLOPS = 2 * V * E * N * (R + 1)
 
 GROUPS = ((0, 1, 2), (3,), (4,), (5,), (6,), (7,))
-AHEAD = 2
+AHEAD = BANKS - 2 * len(GROUPS[0])
 
 F32 = mybir.dt.float32
 BF16 = mybir.dt.bfloat16
@@ -21,9 +22,8 @@ def tile_graphattention_kernel(tc, rel, embed, src_embed, offs, out):
     with (
         tc.tile_pool(name="held", bufs=1) as held,
         tc.tile_pool(name="qpool", bufs=12) as qpool,
-        tc.tile_pool(name="work", bufs=3) as work,
-        tc.psum_pool(name="setup_ps", bufs=AHEAD) as setup_ps,
-        tc.psum_pool(name="acc_ps", bufs=6) as acc_ps,
+        tc.tile_pool(name="work", bufs=5) as work,
+        tc.psum_pool(name="psum", bufs=BANKS) as psum,
     ):
         offsets = held.tile([P, N // 16], U16, name="offsets")
         nc.sync.dma_start(offsets[:], offs)
@@ -46,47 +46,57 @@ def tile_graphattention_kernel(tc, rel, embed, src_embed, offs, out):
 
         embT = held.tile([E, V], BF16, name="embT")
         for first in range(0, VB, 4):
-            embT_ps = setup_ps.tile([E, 4 * P], BF16, name="embT_ps", tag="setup")
+            embT_ps = psum.tile([E, 4 * P], BF16, name="embT_ps", tag="bank")
             for k in range(4):
                 nc.tensor.transpose(embT_ps[:, k * P : (k + 1) * P], embed_sb[:, first + k, :], ident[:])
             nc.vector.tensor_copy(embT[:, first * P : (first + 4) * P], embT_ps[:])
         embed_sum = held.tile([E, 1], F32, name="embed_sum")
         nc.vector.reduce_sum(embed_sum[:], embT[:], axis=mybir.AxisListType.X)
 
-        picked = {}
+        expo = {}
         gain = {}
+        picked = {}
+        recip = {}
 
-        def prepare_block(b):
-            base_ps = setup_ps.tile([P, N], F32, name="base_ps", tag="setup")
+        def start_block(b):
+            base_ps = psum.tile([P, N], F32, name="base_ps", tag="bank")
             nc.tensor.matmul(base_ps[:], embT[:, b * P : (b + 1) * P], src_sb[:], start=True, stop=True)
-            expo = work.tile([P, N], F32, name="expo")
-            nc.scalar.activation(expo[:], base_ps[:], ACT.Exp)
-            gain[b] = held.tile([P, N], F32, name=f"gain{b}")
-            nc.vector.tensor_scalar_add(gain[b][:], expo[:], -1.0)
+            expo[b] = work.tile([P, N], F32, name="expo")
+            nc.scalar.activation(expo[b][:], base_ps[:], ACT.Exp)
             picked[b] = held.tile([P, N], F32, name=f"picked{b}")
             nc.scalar.activation(picked[b][:], rel_sb[b][:].indirect(offsets[:]), ACT.Copy)
 
-        def finish(r, num_ps, den_ps):
+        def invert(r):
             rsqrt = work.tile([P, N], F32, name="rsqrt")
-            nc.scalar.activation(rsqrt[:], den_ps[:], ACT.Abs_reciprocal_sqrt, bias=float(V))
-            num = work.tile([E, N], F32, name="num")
-            nc.scalar.activation(num[:], num_ps[:], ACT.Identity, bias=embed_sum[:, 0:1])
-            recip = work.tile([P, N], F32, name="recip")
-            nc.scalar.activation(recip[:], rsqrt[:], ACT.Square)
+            nc.scalar.activation(rsqrt[:], den_ps[r][:], ACT.Abs_reciprocal_sqrt, bias=float(V))
+            recip[r] = work.tile([P, N], F32, name="recip")
+            nc.scalar.activation(recip[r][:], rsqrt[:], ACT.Square)
+
+        def divide(r):
             res = work.tile([E, N], F32, name="res")
-            nc.vector.tensor_tensor(res[:], num[:], recip[:], ALU.mult)
+            nc.vector.scalar_tensor_tensor(
+                res[:], num_ps[r][:], embed_sum[:, 0:1], recip[r][:], ALU.add, ALU.mult
+            )
             nc.sync.dma_start(out[r * E : (r + 1) * E, :], res[:])
 
         for b in range(AHEAD):
-            prepare_block(b)
+            start_block(b)
+
+        den_ps = {}
+        num_ps = {}
+        summed = ()
         for group in GROUPS:
-            den_ps = {r: acc_ps.tile([P, N], F32, name="bank") for r in group}
-            num_ps = {r: acc_ps.tile([E, N], F32, name="bank") for r in group}
+            for r in group:
+                den_ps[r] = psum.tile([P, N], F32, name="den_ps", tag="bank")
+                num_ps[r] = psum.tile([E, N], F32, name="num_ps", tag="bank")
             for b in range(VB):
-                if group == GROUPS[0] and b + AHEAD < VB:
-                    prepare_block(b + AHEAD)
-                if group == GROUPS[0] and b + AHEAD == VB:
-                    nc.scalar.activation(warm[:, 2:3], warm[:, 0:1], ACT.Abs_reciprocal_sqrt)
+                if group == GROUPS[0]:
+                    if b + AHEAD < VB:
+                        start_block(b + AHEAD)
+                    if b + AHEAD == VB:
+                        nc.scalar.activation(warm[:, 2:3], warm[:, 0:1], ACT.Abs_reciprocal_sqrt)
+                    gain[b] = held.tile([P, N], F32, name=f"gain{b}")
+                    nc.vector.tensor_scalar_add(gain[b][:], expo[b][:], -1.0)
                 for r in group:
                     q = qpool.tile([P, N], BF16, name="q")
                     nc.vector.scalar_tensor_tensor(
@@ -94,5 +104,10 @@ def tile_graphattention_kernel(tc, rel, embed, src_embed, offs, out):
                     )
                     nc.tensor.matmul(den_ps[r][:], ones[:], q[:], start=(b == 0), stop=(b == VB - 1))
                     nc.tensor.matmul(num_ps[r][:], embed_sb[:, b, :], q[:], start=(b == 0), stop=(b == VB - 1))
+            for r in summed:
+                divide(r)
             for r in group:
-                finish(r, num_ps[r], den_ps[r])
+                invert(r)
+            summed = group
+        for r in summed:
+            divide(r)

@@ -4,11 +4,10 @@ from concourse.masks import make_identity
 V, S, E, R, N = 1024, 1024, 128, 8, 512
 P = 128
 VB = V // P
-BANKS = 8
 FLOPS = 2 * V * E * N * (R + 1)
 
 GROUPS = ((0, 1, 2), (3,), (4,), (5,), (6,), (7,))
-AHEAD = BANKS - 2 * len(GROUPS[0])
+AHEAD = 2
 
 F32 = mybir.dt.float32
 BF16 = mybir.dt.bfloat16
@@ -21,9 +20,10 @@ def tile_graphattention_kernel(tc, rel, embed, src_embed, offs, out):
     nc = tc.nc
     with (
         tc.tile_pool(name="held", bufs=1) as held,
-        tc.tile_pool(name="qpool", bufs=12) as qpool,
+        tc.tile_pool(name="qpool", bufs=24) as qpool,
         tc.tile_pool(name="work", bufs=5) as work,
-        tc.psum_pool(name="psum", bufs=BANKS) as psum,
+        tc.psum_pool(name="setup_ps", bufs=AHEAD) as setup_ps,
+        tc.psum_pool(name="acc_ps", bufs=6) as acc_ps,
     ):
         offsets = held.tile([P, N // 16], U16, name="offsets")
         nc.sync.dma_start(offsets[:], offs)
@@ -35,36 +35,43 @@ def tile_graphattention_kernel(tc, rel, embed, src_embed, offs, out):
         for b in range(VB):
             nc.sync.dma_start(rel_sb[b][:], rel[b * P : (b + 1) * P, :])
 
-        warm = held.tile([P, 3], F32, name="warm")
+        warm = held.tile([P, 2], F32, name="warm")
         nc.vector.memset(warm[:, 0:1], 1.0)
         nc.scalar.activation(warm[:, 1:2], warm[:, 0:1], ACT.Exp)
 
         ident = held.tile([P, P], BF16, name="ident")
         make_identity(nc, ident[:])
-        ones = held.tile([P, P], BF16, name="ones")
+        ones = held.tile([P, N], BF16, name="ones")
         nc.gpsimd.memset(ones[:], 1.0)
+
+        idle_ps = setup_ps.tile([P, N], F32, name="idle_ps", tag="setup")
+        for k in range(4):
+            nc.tensor.matmul(idle_ps[:], ones[:, 0:P], ones[:], start=True, stop=True)
 
         embT = held.tile([E, V], BF16, name="embT")
         for first in range(0, VB, 4):
-            embT_ps = psum.tile([E, 4 * P], BF16, name="embT_ps", tag="bank")
+            embT_ps = setup_ps.tile([E, 4 * P], BF16, name="embT_ps", tag="setup")
             for k in range(4):
                 nc.tensor.transpose(embT_ps[:, k * P : (k + 1) * P], embed_sb[:, first + k, :], ident[:])
             nc.vector.tensor_copy(embT[:, first * P : (first + 4) * P], embT_ps[:])
-        embed_sum = held.tile([E, 1], F32, name="embed_sum")
-        nc.vector.reduce_sum(embed_sum[:], embT[:], axis=mybir.AxisListType.X)
 
         expo = {}
         gain = {}
         picked = {}
+        num = {}
         recip = {}
 
         def start_block(b):
-            base_ps = psum.tile([P, N], F32, name="base_ps", tag="bank")
+            base_ps = setup_ps.tile([P, N], F32, name="base_ps", tag="setup")
             nc.tensor.matmul(base_ps[:], embT[:, b * P : (b + 1) * P], src_sb[:], start=True, stop=True)
-            expo[b] = work.tile([P, N], F32, name="expo")
-            nc.scalar.activation(expo[b][:], base_ps[:], ACT.Exp)
             picked[b] = held.tile([P, N], F32, name=f"picked{b}")
             nc.scalar.activation(picked[b][:], rel_sb[b][:].indirect(offsets[:]), ACT.Copy)
+            expo[b] = work.tile([P, N], F32, name="expo")
+            nc.scalar.activation(expo[b][:], base_ps[:], ACT.Exp)
+
+        def evacuate(r):
+            num[r] = work.tile([E, N], F32, name="num")
+            nc.scalar.activation(num[r][:], num_ps[r][:], ACT.Identity, bias=embed_sum[:, 0:1])
 
         def invert(r):
             rsqrt = work.tile([P, N], F32, name="rsqrt")
@@ -74,27 +81,29 @@ def tile_graphattention_kernel(tc, rel, embed, src_embed, offs, out):
 
         def divide(r):
             res = work.tile([E, N], F32, name="res")
-            nc.vector.scalar_tensor_tensor(
-                res[:], num_ps[r][:], embed_sum[:, 0:1], recip[r][:], ALU.add, ALU.mult
-            )
+            nc.vector.tensor_tensor(res[:], num[r][:], recip[r][:], ALU.mult)
             nc.sync.dma_start(out[r * E : (r + 1) * E, :], res[:])
 
         for b in range(AHEAD):
             start_block(b)
+
+        esum_ps = acc_ps.tile([E, N], F32, name="esum_ps", tag="bank")
+        for b in range(VB):
+            nc.tensor.matmul(esum_ps[:, 0:1], embed_sb[:, b, :], ones[:, 0:1], start=(b == 0), stop=(b == VB - 1))
+        embed_sum = held.tile([E, 1], F32, name="embed_sum")
+        nc.vector.tensor_copy(embed_sum[:], esum_ps[:, 0:1])
 
         den_ps = {}
         num_ps = {}
         summed = ()
         for group in GROUPS:
             for r in group:
-                den_ps[r] = psum.tile([P, N], F32, name="den_ps", tag="bank")
-                num_ps[r] = psum.tile([E, N], F32, name="num_ps", tag="bank")
+                den_ps[r] = acc_ps.tile([P, N], F32, name="den_ps", tag="bank")
+                num_ps[r] = acc_ps.tile([E, N], F32, name="num_ps", tag="bank")
             for b in range(VB):
                 if group == GROUPS[0]:
                     if b + AHEAD < VB:
                         start_block(b + AHEAD)
-                    if b + AHEAD == VB:
-                        nc.scalar.activation(warm[:, 2:3], warm[:, 0:1], ACT.Abs_reciprocal_sqrt)
                     gain[b] = held.tile([P, N], F32, name=f"gain{b}")
                     nc.vector.tensor_scalar_add(gain[b][:], expo[b][:], -1.0)
                 for r in group:
@@ -102,10 +111,12 @@ def tile_graphattention_kernel(tc, rel, embed, src_embed, offs, out):
                     nc.vector.scalar_tensor_tensor(
                         q[:], picked[b][:], float(r + 1), gain[b][:], ALU.is_equal, ALU.mult
                     )
-                    nc.tensor.matmul(den_ps[r][:], ones[:], q[:], start=(b == 0), stop=(b == VB - 1))
+                    nc.tensor.matmul(den_ps[r][:], ones[:, 0:P], q[:], start=(b == 0), stop=(b == VB - 1))
                     nc.tensor.matmul(num_ps[r][:], embed_sb[:, b, :], q[:], start=(b == 0), stop=(b == VB - 1))
             for r in summed:
                 divide(r)
+            for r in group:
+                evacuate(r)
             for r in group:
                 invert(r)
             summed = group

@@ -49,11 +49,17 @@ def tile_graphattention_kernel(tc, rel, embed, src_embed, offs, out):
             nc.tensor.matmul(idle_ps[:], ones[:, 0:P], ones[:], start=True, stop=True)
 
         embT = held.tile([E, V], BF16, name="embT")
-        for first in range(0, VB, 4):
+        half_sum = held.tile([E, 2], F32, name="half_sum")
+        for h in range(2):
             embT_ps = setup_ps.tile([E, 4 * P], BF16, name="embT_ps", tag="setup")
             for k in range(4):
-                nc.tensor.transpose(embT_ps[:, k * P : (k + 1) * P], embed_sb[:, first + k, :], ident[:])
-            nc.vector.tensor_copy(embT[:, first * P : (first + 4) * P], embT_ps[:])
+                nc.tensor.transpose(embT_ps[:, k * P : (k + 1) * P], embed_sb[:, 4 * h + k, :], ident[:])
+            nc.vector.tensor_copy(embT[:, 4 * h * P : 4 * (h + 1) * P], embT_ps[:])
+            nc.vector.reduce_sum(
+                half_sum[:, h : h + 1], embT[:, 4 * h * P : 4 * (h + 1) * P], axis=mybir.AxisListType.X
+            )
+        embed_sum = held.tile([E, 1], F32, name="embed_sum")
+        nc.vector.tensor_add(embed_sum[:], half_sum[:, 0:1], half_sum[:, 1:2])
 
         expo = {}
         gain = {}
@@ -71,7 +77,7 @@ def tile_graphattention_kernel(tc, rel, embed, src_embed, offs, out):
 
         def evacuate(r):
             num[r] = work.tile([E, N], F32, name="num")
-            nc.scalar.activation(num[r][:], num_ps[r][:], ACT.Identity, bias=embed_sum[:, 0:1])
+            nc.scalar.copy(num[r][:], num_ps[r][:])
 
         def invert(r):
             rsqrt = work.tile([P, N], F32, name="rsqrt")
@@ -81,17 +87,11 @@ def tile_graphattention_kernel(tc, rel, embed, src_embed, offs, out):
 
         def divide(r):
             res = work.tile([E, N], F32, name="res")
-            nc.vector.tensor_tensor(res[:], num[r][:], recip[r][:], ALU.mult)
+            nc.vector.scalar_tensor_tensor(res[:], num[r][:], embed_sum[:, 0:1], recip[r][:], ALU.add, ALU.mult)
             nc.sync.dma_start(out[r * E : (r + 1) * E, :], res[:])
 
         for b in range(AHEAD):
             start_block(b)
-
-        esum_ps = acc_ps.tile([E, N], F32, name="esum_ps", tag="bank")
-        for b in range(VB):
-            nc.tensor.matmul(esum_ps[:, 0:1], embed_sb[:, b, :], ones[:, 0:1], start=(b == 0), stop=(b == VB - 1))
-        embed_sum = held.tile([E, 1], F32, name="embed_sum")
-        nc.vector.tensor_copy(embed_sum[:], esum_ps[:, 0:1])
 
         den_ps = {}
         num_ps = {}
@@ -116,7 +116,10 @@ def tile_graphattention_kernel(tc, rel, embed, src_embed, offs, out):
             for r in summed:
                 divide(r)
             for r in group:
-                evacuate(r)
+                if group == GROUPS[0]:
+                    evacuate(r)
+                else:
+                    num[r] = num_ps[r]
             for r in group:
                 invert(r)
             summed = group

@@ -21,6 +21,7 @@ def tile_graphattention_kernel(tc, rel, embed, src_embed, offs, out):
     with (
         tc.tile_pool(name="held", bufs=1) as held,
         tc.tile_pool(name="qpool", bufs=24) as qpool,
+        tc.tile_pool(name="maskpool", bufs=4) as maskpool,
         tc.tile_pool(name="work", bufs=5) as work,
         tc.psum_pool(name="setup_ps", bufs=AHEAD) as setup_ps,
         tc.psum_pool(name="acc_ps", bufs=6) as acc_ps,
@@ -63,6 +64,7 @@ def tile_graphattention_kernel(tc, rel, embed, src_embed, offs, out):
 
         expo = {}
         gain = {}
+        looked_up = {}
         picked = {}
         num = {}
         recip = {}
@@ -70,8 +72,8 @@ def tile_graphattention_kernel(tc, rel, embed, src_embed, offs, out):
         def start_block(b):
             base_ps = setup_ps.tile([P, N], F32, name="base_ps", tag="setup")
             nc.tensor.matmul(base_ps[:], embT[:, b * P : (b + 1) * P], src_sb[:], start=True, stop=True)
-            picked[b] = held.tile([P, N], F32, name=f"picked{b}")
-            nc.scalar.activation(picked[b][:], rel_sb[b][:].indirect(offsets[:]), ACT.Copy)
+            looked_up[b] = work.tile([P, N], F32, name="looked_up")
+            nc.scalar.activation(looked_up[b][:], rel_sb[b][:].indirect(offsets[:]), ACT.Copy)
             expo[b] = work.tile([P, N], F32, name="expo")
             nc.scalar.activation(expo[b][:], base_ps[:], ACT.Exp)
 
@@ -104,13 +106,15 @@ def tile_graphattention_kernel(tc, rel, embed, src_embed, offs, out):
                 if group == GROUPS[0]:
                     if b + AHEAD < VB:
                         start_block(b + AHEAD)
-                    gain[b] = held.tile([P, N], F32, name=f"gain{b}")
-                    nc.vector.tensor_scalar_add(gain[b][:], expo[b][:], -1.0)
+                    picked[b] = held.tile([P, N], BF16, name=f"picked{b}")
+                    nc.vector.tensor_copy(picked[b][:], looked_up[b][:])
+                    gain[b] = held.tile([P, N], BF16, name=f"gain{b}")
+                    nc.vector.tensor_scalar(gain[b][:], expo[b][:], -1.0, 3.0e38, op0=ALU.add, op1=ALU.min)
                 for r in group:
+                    mask = maskpool.tile([P, N], BF16, name="mask")
+                    nc.vector.tensor_single_scalar(mask[:], picked[b][:], float(r + 1), op=ALU.is_equal)
                     q = qpool.tile([P, N], BF16, name="q")
-                    nc.vector.scalar_tensor_tensor(
-                        q[:], picked[b][:], float(r + 1), gain[b][:], ALU.is_equal, ALU.mult
-                    )
+                    nc.vector.tensor_mul(q[:], mask[:], gain[b][:])
                     nc.tensor.matmul(den_ps[r][:], ones[:, 0:P], q[:], start=(b == 0), stop=(b == VB - 1))
                     nc.tensor.matmul(num_ps[r][:], embed_sb[:, b, :], q[:], start=(b == 0), stop=(b == VB - 1))
             for r in summed:

@@ -4,10 +4,12 @@ from concourse.masks import make_identity
 V, S, E, R, N = 1024, 1024, 128, 8, 512
 P = 128
 VB = V // P
+JC = N // P
 FLOPS = 2 * V * E * N * (R + 1)
-
-GROUPS = ((0, 1, 2), (3,), (4,), (5,), (6,), (7,))
 AHEAD = 2
+W = E + 2
+PITCH = 144
+FIRST = 3
 
 F32 = mybir.dt.float32
 BF16 = mybir.dt.bfloat16
@@ -22,14 +24,15 @@ def tile_graphattention_kernel(tc, rel, embed, src_embed, offs, out):
         tc.tile_pool(name="held", bufs=1) as held,
         tc.tile_pool(name="qpool", bufs=24) as qpool,
         tc.tile_pool(name="maskpool", bufs=4) as maskpool,
-        tc.tile_pool(name="work", bufs=5) as work,
+        tc.tile_pool(name="work", bufs=4) as work,
         tc.psum_pool(name="setup_ps", bufs=AHEAD) as setup_ps,
-        tc.psum_pool(name="acc_ps", bufs=6) as acc_ps,
+        tc.psum_pool(name="sums_ps", bufs=2 * FIRST) as sums_ps,
     ):
         offsets = held.tile([P, N // 16], U16, name="offsets")
         nc.sync.dma_start(offsets[:], offs)
-        embed_sb = held.tile([P, VB, E], BF16, name="embed_sb")
-        nc.sync.dma_start(embed_sb[:], embed.rearrange("(b p) e -> p b e", p=P))
+        embed_ones = held.tile([P, VB, PITCH], BF16, name="embed_ones")
+        nc.sync.dma_start(embed_ones[:, :, 0:E], embed.rearrange("(b p) e -> p b e", p=P))
+        nc.gpsimd.memset(embed_ones[:, :, E:W], 1.0)
         src_sb = held.tile([E, N], BF16, name="src_sb")
         nc.sync.dma_start(src_sb[:], src_embed)
         rel_sb = [held.tile([P, S], F32, name=f"rel{b}") for b in range(VB)]
@@ -42,32 +45,40 @@ def tile_graphattention_kernel(tc, rel, embed, src_embed, offs, out):
 
         ident = held.tile([P, P], BF16, name="ident")
         make_identity(nc, ident[:])
+        ident_f32 = held.tile([P, P], F32, name="ident_f32")
+        make_identity(nc, ident_f32[:])
         ones = held.tile([P, N], BF16, name="ones")
         nc.gpsimd.memset(ones[:], 1.0)
 
         idle_ps = setup_ps.tile([P, N], F32, name="idle_ps", tag="setup")
-        for k in range(4):
+        for i in range(4):
             nc.tensor.matmul(idle_ps[:], ones[:, 0:P], ones[:], start=True, stop=True)
 
         embT = held.tile([E, V], BF16, name="embT")
-        half_sum = held.tile([E, 2], F32, name="half_sum")
         for h in range(2):
             embT_ps = setup_ps.tile([E, 4 * P], BF16, name="embT_ps", tag="setup")
-            for k in range(4):
-                nc.tensor.transpose(embT_ps[:, k * P : (k + 1) * P], embed_sb[:, 4 * h + k, :], ident[:])
+            for i in range(4):
+                nc.tensor.transpose(embT_ps[:, i * P : (i + 1) * P], embed_ones[:, 4 * h + i, 0:E], ident[:])
             nc.vector.tensor_copy(embT[:, 4 * h * P : 4 * (h + 1) * P], embT_ps[:])
-            nc.vector.reduce_sum(
-                half_sum[:, h : h + 1], embT[:, 4 * h * P : 4 * (h + 1) * P], axis=mybir.AxisListType.X
-            )
-        embed_sum = held.tile([E, 1], F32, name="embed_sum")
-        nc.vector.tensor_add(embed_sum[:], half_sum[:, 0:1], half_sum[:, 1:2])
+
+        colsum_ps = setup_ps.tile([P, W], F32, name="colsum_ps", tag="setup")
+        for b in range(VB):
+            nc.tensor.matmul(colsum_ps[:], ones[:, 0:P], embed_ones[:, b, 0:W], start=(b == 0), stop=(b == VB - 1))
+        rounded = held.tile([P, W], BF16, name="rounded")
+        nc.vector.tensor_copy(rounded[:], colsum_ps[:])
+        rest = held.tile([P, W], BF16, name="rest")
+        nc.vector.tensor_sub(rest[:], colsum_ps[:], rounded[:])
+        H = P // 2
+        opening = held.tile([P, 2, W], BF16, name="opening")
+        for i in range(2):
+            nc.vector.tensor_scalar_mul(opening[0:H, i, :], rounded[0:H, :], 1.0 / H)
+            nc.vector.tensor_scalar_mul(opening[H:P, i, :], rest[H:P, :], 1.0 / H)
 
         expo = {}
         gain = {}
         looked_up = {}
         picked = {}
-        num = {}
-        recip = {}
+        sums = {}
 
         def start_block(b):
             base_ps = setup_ps.tile([P, N], F32, name="base_ps", tag="setup")
@@ -77,55 +88,70 @@ def tile_graphattention_kernel(tc, rel, embed, src_embed, offs, out):
             expo[b] = work.tile([P, N], F32, name="expo")
             nc.scalar.activation(expo[b][:], base_ps[:], ACT.Exp)
 
-        def evacuate(r):
-            num[r] = work.tile([E, N], F32, name="num")
-            nc.scalar.copy(num[r][:], num_ps[r][:])
+        def open_banks(r):
+            sums[r] = []
+            for h in range(JC // 2):
+                bank = sums_ps.tile([P, 2, W], F32, name="bank")
+                nc.tensor.matmul(bank[:], ones[:, 0:P], opening[:], start=True, stop=False)
+                sums[r].append(bank)
 
-        def invert(r):
-            rsqrt = work.tile([P, N], F32, name="rsqrt")
-            nc.scalar.activation(rsqrt[:], den_ps[r][:], ACT.Abs_reciprocal_sqrt, bias=float(V))
-            recip[r] = work.tile([P, N], F32, name="recip")
-            nc.scalar.activation(recip[r][:], rsqrt[:], ACT.Square)
+        def add_block(r, b):
+            mask = maskpool.tile([P, N], BF16, name="mask")
+            nc.vector.tensor_single_scalar(mask[:], picked[b][:], float(r + 1), op=ALU.is_equal)
+            q = qpool.tile([P, N], BF16, name="q")
+            nc.vector.tensor_mul(q[:], mask[:], gain[b][:])
+            for c in range(JC):
+                nc.tensor.matmul(
+                    sums[r][c // 2][:, c % 2, :],
+                    q[:, c * P : (c + 1) * P],
+                    embed_ones[:, b, 0:W],
+                    start=False,
+                    stop=(b == VB - 1 and c % 2 == 1),
+                )
 
         def divide(r):
+            quot = work.tile([P, JC, E], F32, name="quot")
+            for h in range(JC // 2):
+                rsqrt = work.tile([P, 2, 1], F32, name="rsqrt")
+                nc.scalar.activation(rsqrt[:], sums[r][h][:, :, E : E + 1], ACT.Abs_reciprocal_sqrt)
+                recip = work.tile([P, 2, 1], F32, name="recip")
+                nc.scalar.activation(recip[:], rsqrt[:], ACT.Square)
+                for i in range(2):
+                    nc.scalar.activation(
+                        quot[:, 2 * h + i, :], sums[r][h][:, i, 0:E], ACT.Identity, scale=recip[:, i, :]
+                    )
+            return quot
+
+        def turn_back(r, quot):
+            out_ps = setup_ps.tile([E, N], F32, name="out_ps", tag="setup")
+            for c in range(JC):
+                nc.tensor.transpose(out_ps[:, c * P : (c + 1) * P], quot[:, c, :], ident_f32[:])
             res = work.tile([E, N], F32, name="res")
-            nc.vector.scalar_tensor_tensor(res[:], num[r][:], embed_sum[:, 0:1], recip[r][:], ALU.add, ALU.mult)
+            nc.scalar.copy(res[:], out_ps[:])
             nc.sync.dma_start(out[r * E : (r + 1) * E, :], res[:])
 
         for b in range(AHEAD):
             start_block(b)
 
-        den_ps = {}
-        num_ps = {}
-        summed = ()
-        for group in GROUPS:
-            for r in group:
-                den_ps[r] = acc_ps.tile([P, N], F32, name="den_ps", tag="bank")
-                num_ps[r] = acc_ps.tile([E, N], F32, name="num_ps", tag="bank")
+        for r in range(FIRST):
+            open_banks(r)
+        for b in range(VB):
+            if b + AHEAD < VB:
+                start_block(b + AHEAD)
+            picked[b] = held.tile([P, N], BF16, name=f"picked{b}")
+            nc.vector.tensor_copy(picked[b][:], looked_up[b][:])
+            gain[b] = held.tile([P, N], BF16, name=f"gain{b}")
+            nc.vector.tensor_scalar(gain[b][:], expo[b][:], -1.0, 3.0e38, op0=ALU.add, op1=ALU.min)
+            for r in range(FIRST):
+                add_block(r, b)
+        divided = [(r, divide(r)) for r in range(FIRST)]
+
+        for r in range(FIRST, R):
+            open_banks(r)
             for b in range(VB):
-                if group == GROUPS[0]:
-                    if b + AHEAD < VB:
-                        start_block(b + AHEAD)
-                    picked[b] = held.tile([P, N], BF16, name=f"picked{b}")
-                    nc.vector.tensor_copy(picked[b][:], looked_up[b][:])
-                    gain[b] = held.tile([P, N], BF16, name=f"gain{b}")
-                    nc.vector.tensor_scalar(gain[b][:], expo[b][:], -1.0, 3.0e38, op0=ALU.add, op1=ALU.min)
-                for r in group:
-                    mask = maskpool.tile([P, N], BF16, name="mask")
-                    nc.vector.tensor_single_scalar(mask[:], picked[b][:], float(r + 1), op=ALU.is_equal)
-                    q = qpool.tile([P, N], BF16, name="q")
-                    nc.vector.tensor_mul(q[:], mask[:], gain[b][:])
-                    nc.tensor.matmul(den_ps[r][:], ones[:, 0:P], q[:], start=(b == 0), stop=(b == VB - 1))
-                    nc.tensor.matmul(num_ps[r][:], embed_sb[:, b, :], q[:], start=(b == 0), stop=(b == VB - 1))
-            for r in summed:
-                divide(r)
-            for r in group:
-                if group == GROUPS[0]:
-                    evacuate(r)
-                else:
-                    num[r] = num_ps[r]
-            for r in group:
-                invert(r)
-            summed = group
-        for r in summed:
-            divide(r)
+                add_block(r, b)
+                if b % 2 == 1 and divided:
+                    turn_back(*divided.pop(0))
+            divided.append((r, divide(r)))
+        for r, quot in divided:
+            turn_back(r, quot)

@@ -9,7 +9,10 @@ FLOPS = 2 * V * E * N * (R + 1)
 AHEAD = 2
 W = E + 2
 PITCH = 144
+HB = VB // 2
 FIRST = 3
+GROUP = 2
+TILES = max(FIRST, GROUP)
 
 F32 = mybir.dt.float32
 BF16 = mybir.dt.bfloat16
@@ -22,8 +25,8 @@ def tile_graphattention_kernel(tc, rel, embed, src_embed, offs, out):
     nc = tc.nc
     with (
         tc.tile_pool(name="held", bufs=1) as held,
-        tc.tile_pool(name="qpool", bufs=24) as qpool,
-        tc.tile_pool(name="maskpool", bufs=4) as maskpool,
+        tc.tile_pool(name="qpool", bufs=8) as qpool,
+        tc.tile_pool(name="maskpool", bufs=3) as maskpool,
         tc.tile_pool(name="work", bufs=4) as work,
         tc.psum_pool(name="setup_ps", bufs=AHEAD) as setup_ps,
         tc.psum_pool(name="sums_ps", bufs=2 * FIRST) as sums_ps,
@@ -31,37 +34,60 @@ def tile_graphattention_kernel(tc, rel, embed, src_embed, offs, out):
         offsets = held.tile([P, N // 16], U16, name="offsets")
         nc.sync.dma_start(offsets[:], offs)
         embed_ones = held.tile([P, VB, PITCH], BF16, name="embed_ones")
-        nc.sync.dma_start(embed_ones[:, :, 0:E], embed.rearrange("(b p) e -> p b e", p=P))
-        nc.gpsimd.memset(embed_ones[:, :, E:W], 1.0)
+        embed_blocks = embed.rearrange("(b p) e -> p b e", p=P)
         src_sb = held.tile([E, N], BF16, name="src_sb")
-        nc.sync.dma_start(src_sb[:], src_embed)
         rel_sb = [held.tile([P, S], F32, name=f"rel{b}") for b in range(VB)]
-        for b in range(VB):
+        nc.sync.dma_start(embed_ones[:, 0:HB, 0:E], embed_blocks[:, 0:HB, :])
+        nc.sync.dma_start(src_sb[:], src_embed)
+        nc.sync.dma_start(rel_sb[0][:], rel[0:P, :])
+        nc.sync.dma_start(embed_ones[:, HB:VB, 0:E], embed_blocks[:, HB:VB, :])
+        for b in range(1, VB):
             nc.sync.dma_start(rel_sb[b][:], rel[b * P : (b + 1) * P, :])
+        nc.gpsimd.memset(embed_ones[:, :, E:W], 1.0)
 
         warm = held.tile([P, 2], F32, name="warm")
         nc.vector.memset(warm[:, 0:1], 1.0)
         nc.scalar.activation(warm[:, 1:2], warm[:, 0:1], ACT.Exp)
 
+        ones = held.tile([P, N], BF16, name="ones")
+        nc.gpsimd.memset(ones[:], 1.0)
         ident = held.tile([P, P], BF16, name="ident")
         make_identity(nc, ident[:])
         ident_f32 = held.tile([P, P], F32, name="ident_f32")
         make_identity(nc, ident_f32[:])
-        ones = held.tile([P, N], BF16, name="ones")
-        nc.gpsimd.memset(ones[:], 1.0)
 
-        idle_ps = setup_ps.tile([P, N], F32, name="idle_ps", tag="setup")
+        expo = {}
+        looked_up = {}
+        gain = held.tile([P, VB, N], BF16, name="gain")
+        picked = held.tile([P, VB, N], BF16, name="picked")
+        finished = []
+        mask_of = {}
+        sums = {}
+
+        def start_block(b):
+            base_ps = setup_ps.tile([P, N], F32, name="base_ps", tag="setup")
+            nc.tensor.matmul(base_ps[:], embT[:, b * P : (b + 1) * P], src_sb[:], start=True, stop=True)
+            expo[b] = work.tile([P, N], F32, name="expo")
+            nc.scalar.activation(expo[b][:], base_ps[:], ACT.Exp)
+            looked_up[b] = work.tile([P, N], F32, name="looked_up")
+            nc.scalar.activation(looked_up[b][:], rel_sb[b][:].indirect(offsets[:]), ACT.Copy)
+
+
+        idle_ps = sums_ps.tile([P, N], F32, name="idle_ps", tag="bank")
         for i in range(4):
             nc.tensor.matmul(idle_ps[:], ones[:, 0:P], ones[:], start=True, stop=True)
 
         embT = held.tile([E, V], BF16, name="embT")
         for h in range(2):
-            embT_ps = setup_ps.tile([E, 4 * P], BF16, name="embT_ps", tag="setup")
-            for i in range(4):
-                nc.tensor.transpose(embT_ps[:, i * P : (i + 1) * P], embed_ones[:, 4 * h + i, 0:E], ident[:])
-            nc.vector.tensor_copy(embT[:, 4 * h * P : 4 * (h + 1) * P], embT_ps[:])
+            embT_ps = sums_ps.tile([E, HB * P], BF16, name="embT_ps", tag="bank")
+            for i in range(HB):
+                nc.tensor.transpose(embT_ps[:, i * P : (i + 1) * P], embed_ones[:, HB * h + i, 0:E], ident[:])
+            nc.vector.tensor_copy(embT[:, HB * h * P : HB * (h + 1) * P], embT_ps[:])
+            if h == 0:
+                for b in range(AHEAD):
+                    start_block(b)
 
-        colsum_ps = setup_ps.tile([P, W], F32, name="colsum_ps", tag="setup")
+        colsum_ps = sums_ps.tile([P, W], F32, name="colsum_ps", tag="bank")
         for b in range(VB):
             nc.tensor.matmul(colsum_ps[:], ones[:, 0:P], embed_ones[:, b, 0:W], start=(b == 0), stop=(b == VB - 1))
         rounded = held.tile([P, W], BF16, name="rounded")
@@ -74,40 +100,48 @@ def tile_graphattention_kernel(tc, rel, embed, src_embed, offs, out):
             nc.vector.tensor_scalar_mul(opening[0:H, i, :], rounded[0:H, :], 1.0 / H)
             nc.vector.tensor_scalar_mul(opening[H:P, i, :], rest[H:P, :], 1.0 / H)
 
-        expo = {}
-        gain = {}
-        looked_up = {}
-        picked = {}
-        sums = {}
-
-        def start_block(b):
-            base_ps = setup_ps.tile([P, N], F32, name="base_ps", tag="setup")
-            nc.tensor.matmul(base_ps[:], embT[:, b * P : (b + 1) * P], src_sb[:], start=True, stop=True)
-            looked_up[b] = work.tile([P, N], F32, name="looked_up")
-            nc.scalar.activation(looked_up[b][:], rel_sb[b][:].indirect(offsets[:]), ACT.Copy)
-            expo[b] = work.tile([P, N], F32, name="expo")
-            nc.scalar.activation(expo[b][:], base_ps[:], ACT.Exp)
-
         def open_banks(r):
             sums[r] = []
             for h in range(JC // 2):
-                bank = sums_ps.tile([P, 2, W], F32, name="bank")
+                bank = sums_ps.tile([P, 2, W], F32, name="bank", tag="bank")
                 nc.tensor.matmul(bank[:], ones[:, 0:P], opening[:], start=True, stop=False)
                 sums[r].append(bank)
 
-        def add_block(r, b):
-            mask = maskpool.tile([P, N], BF16, name="mask")
-            nc.vector.tensor_single_scalar(mask[:], picked[b][:], float(r + 1), op=ALU.is_equal)
-            q = qpool.tile([P, N], BF16, name="q")
-            nc.vector.tensor_mul(q[:], mask[:], gain[b][:])
-            for c in range(JC):
-                nc.tensor.matmul(
-                    sums[r][c // 2][:, c % 2, :],
-                    q[:, c * P : (c + 1) * P],
-                    embed_ones[:, b, 0:W],
-                    start=False,
-                    stop=(b == VB - 1 and c % 2 == 1),
+        def finish_block(b):
+            if b + AHEAD < VB:
+                start_block(b + AHEAD)
+            nc.vector.tensor_scalar(gain[:, b, :], expo[b][:], -1.0, 3.0e38, op0=ALU.add, op1=ALU.min)
+            nc.vector.tensor_copy(picked[:, b, :], looked_up[b][:])
+            finished.append(b)
+
+
+        def make_masks(r0, nr, b0, nb):
+            for b in range(b0, b0 + nb):
+                if b not in finished:
+                    finish_block(b)
+            mask = maskpool.tile([P, TILES, N], BF16, name="mask")
+            for i in range(nr):
+                nc.vector.tensor_single_scalar(
+                    mask[:, i * nb : (i + 1) * nb, :], picked[:, b0 : b0 + nb, :], float(r0 + i + 1), op=ALU.is_equal
                 )
+            mask_of[r0, b0] = mask
+
+        def add_step(r0, nr, b0, nb):
+            q = qpool.tile([P, TILES, N], BF16, name="q")
+            factor = gain[:, b0 : b0 + nb, :]
+            if nr > 1:
+                factor = factor.to_broadcast([P, nr, N])
+            nc.vector.tensor_mul(q[:, 0 : nr * nb, :], mask_of[r0, b0][:, 0 : nr * nb, :], factor)
+            for i in range(nr):
+                for k in range(nb):
+                    for c in range(JC):
+                        nc.tensor.matmul(
+                            sums[r0 + i][c // 2][:, c % 2, :],
+                            q[:, i * nb + k, c * P : (c + 1) * P],
+                            embed_ones[:, b0 + k, 0:W],
+                            start=False,
+                            stop=(b0 + k == VB - 1 and c % 2 == 1),
+                        )
 
         def divide(r):
             quot = work.tile([P, JC, E], F32, name="quot")
@@ -130,28 +164,21 @@ def tile_graphattention_kernel(tc, rel, embed, src_embed, offs, out):
             nc.scalar.copy(res[:], out_ps[:])
             nc.sync.dma_start(out[r * E : (r + 1) * E, :], res[:])
 
-        for b in range(AHEAD):
-            start_block(b)
-
-        for r in range(FIRST):
-            open_banks(r)
-        for b in range(VB):
-            if b + AHEAD < VB:
-                start_block(b + AHEAD)
-            picked[b] = held.tile([P, N], BF16, name=f"picked{b}")
-            nc.vector.tensor_copy(picked[b][:], looked_up[b][:])
-            gain[b] = held.tile([P, N], BF16, name=f"gain{b}")
-            nc.vector.tensor_scalar(gain[b][:], expo[b][:], -1.0, 3.0e38, op0=ALU.add, op1=ALU.min)
-            for r in range(FIRST):
-                add_block(r, b)
-        divided = [(r, divide(r)) for r in range(FIRST)]
-
-        for r in range(FIRST, R):
-            open_banks(r)
-            for b in range(VB):
-                add_block(r, b)
-                if b % 2 == 1 and divided:
-                    turn_back(*divided.pop(0))
-            divided.append((r, divide(r)))
+        steps = [(0, FIRST, b, 1) for b in range(VB)]
+        steps += [(r, 1, b0, GROUP) for r in range(FIRST, R) for b0 in range(0, VB, GROUP)]
+        divided = []
+        make_masks(*steps[0])
+        for s, (r0, nr, b0, nb) in enumerate(steps):
+            if s + 1 < len(steps):
+                make_masks(*steps[s + 1])
+            if b0 == 0:
+                for r in range(r0, r0 + nr):
+                    open_banks(r)
+            add_step(r0, nr, b0, nb)
+            if r0 >= FIRST and s % 2 == 1 and divided:
+                turn_back(*divided.pop(0))
+            if b0 + nb == VB:
+                for r in range(r0, r0 + nr):
+                    divided.append((r, divide(r)))
         for r, quot in divided:
             turn_back(r, quot)

@@ -34,13 +34,14 @@ def tile_graphattention_kernel(tc, rel, embed, src_embed, offs, out):
         offsets = held.tile([P, N // 16], U16, name="offsets")
         nc.sync.dma_start(offsets[:], offs)
         embed_ones = held.tile([P, VB, PITCH], BF16, name="embed_ones")
-        embed_blocks = embed.rearrange("(b p) e -> p b e", p=P)
         src_sb = held.tile([E, N], BF16, name="src_sb")
         rel_sb = [held.tile([P, S], F32, name=f"rel{b}") for b in range(VB)]
-        nc.sync.dma_start(embed_ones[:, 0:HB, 0:E], embed_blocks[:, 0:HB, :])
+        for b in range(HB):
+            nc.sync.dma_start(embed_ones[:, b, 0:E], embed[b * P : (b + 1) * P, :])
         nc.sync.dma_start(src_sb[:], src_embed)
         nc.sync.dma_start(rel_sb[0][:], rel[0:P, :])
-        nc.sync.dma_start(embed_ones[:, HB:VB, 0:E], embed_blocks[:, HB:VB, :])
+        for b in range(HB, VB):
+            nc.sync.dma_start(embed_ones[:, b, 0:E], embed[b * P : (b + 1) * P, :])
         for b in range(1, VB):
             nc.sync.dma_start(rel_sb[b][:], rel[b * P : (b + 1) * P, :])
         nc.gpsimd.memset(embed_ones[:, :, E:W], 1.0)
@@ -67,10 +68,10 @@ def tile_graphattention_kernel(tc, rel, embed, src_embed, offs, out):
         def start_block(b):
             base_ps = setup_ps.tile([P, N], F32, name="base_ps", tag="setup")
             nc.tensor.matmul(base_ps[:], embT[:, b * P : (b + 1) * P], src_sb[:], start=True, stop=True)
-            expo[b] = work.tile([P, N], F32, name="expo")
-            nc.scalar.activation(expo[b][:], base_ps[:], ACT.Exp)
             looked_up[b] = work.tile([P, N], F32, name="looked_up")
             nc.scalar.activation(looked_up[b][:], rel_sb[b][:].indirect(offsets[:]), ACT.Copy)
+            expo[b] = work.tile([P, N], F32, name="expo")
+            nc.scalar.activation(expo[b][:], base_ps[:], ACT.Exp)
 
 
         idle_ps = sums_ps.tile([P, N], F32, name="idle_ps", tag="bank")
@@ -110,8 +111,8 @@ def tile_graphattention_kernel(tc, rel, embed, src_embed, offs, out):
         def finish_block(b):
             if b + AHEAD < VB:
                 start_block(b + AHEAD)
-            nc.vector.tensor_scalar(gain[:, b, :], expo[b][:], -1.0, 3.0e38, op0=ALU.add, op1=ALU.min)
             nc.vector.tensor_copy(picked[:, b, :], looked_up[b][:])
+            nc.vector.tensor_scalar(gain[:, b, :], expo[b][:], -1.0, 3.0e38, op0=ALU.add, op1=ALU.min)
             finished.append(b)
 
 

@@ -74,10 +74,6 @@ def tile_graphattention_kernel(tc, rel, embed, src_embed, offs, out):
             nc.scalar.activation(expo[b][:], base_ps[:], ACT.Exp)
 
 
-        idle_ps = sums_ps.tile([P, N], F32, name="idle_ps", tag="bank")
-        for i in range(4):
-            nc.tensor.matmul(idle_ps[:], ones[:, 0:P], ones[:], start=True, stop=True)
-
         embT = held.tile([E, V], BF16, name="embT")
         for h in range(2):
             embT_ps = sums_ps.tile([E, HB * P], BF16, name="embT_ps", tag="bank")

@@ -143,14 +143,19 @@ def tile_graphattention_kernel(tc, rel, embed, src_embed, offs, out):
         def divide(r):
             quot = work.tile([P, JC, E], F32, name="quot")
             for h in range(JC // 2):
-                rsqrt = work.tile([P, 2, 1], F32, name="rsqrt")
-                nc.scalar.activation(rsqrt[:], sums[r][h][:, :, E : E + 1], ACT.Abs_reciprocal_sqrt)
                 recip = work.tile([P, 2, 1], F32, name="recip")
-                nc.scalar.activation(recip[:], rsqrt[:], ACT.Square)
-                for i in range(2):
-                    nc.scalar.activation(
-                        quot[:, 2 * h + i, :], sums[r][h][:, i, 0:E], ACT.Identity, scale=recip[:, i, :]
-                    )
+                if r == R - 1 and h == 1:
+                    nc.vector.reciprocal(recip[:], sums[r][h][:, :, E : E + 1])
+                    for i in range(2):
+                        nc.vector.tensor_scalar_mul(quot[:, 2 * h + i, :], sums[r][h][:, i, 0:E], recip[:, i, :])
+                else:
+                    rsqrt = work.tile([P, 2, 1], F32, name="rsqrt")
+                    nc.scalar.activation(rsqrt[:], sums[r][h][:, :, E : E + 1], ACT.Abs_reciprocal_sqrt)
+                    nc.scalar.activation(recip[:], rsqrt[:], ACT.Square)
+                    for i in range(2):
+                        nc.scalar.activation(
+                            quot[:, 2 * h + i, :], sums[r][h][:, i, 0:E], ACT.Identity, scale=recip[:, i, :]
+                        )
             return quot
 
         def turn_back(r, quot):

import concourse.mybir as mybir
from concourse.masks import make_identity

V, S, E, R, N = 1024, 1024, 128, 8, 512
P = 128
VB = V // P
JC = N // P
FLOPS = 2 * V * E * N * (R + 1)
AHEAD = 2
W = E + 2
PITCH = 144
HB = VB // 2
FIRST = 3
GROUP = 2
TILES = max(FIRST, GROUP)

F32 = mybir.dt.float32
BF16 = mybir.dt.bfloat16
U16 = mybir.dt.uint16
ACT = mybir.ActivationFunctionType
ALU = mybir.AluOpType


def tile_graphattention_kernel(tc, rel, embed, src_embed, offs, out):
    nc = tc.nc
    with (
        tc.tile_pool(name="held", bufs=1) as held,
        tc.tile_pool(name="qpool", bufs=8) as qpool,
        tc.tile_pool(name="maskpool", bufs=3) as maskpool,
        tc.tile_pool(name="work", bufs=4) as work,
        tc.psum_pool(name="setup_ps", bufs=AHEAD) as setup_ps,
        tc.psum_pool(name="sums_ps", bufs=2 * FIRST) as sums_ps,
    ):
        offsets = held.tile([P, N // 16], U16, name="offsets")
        nc.sync.dma_start(offsets[:], offs)
        embed_ones = held.tile([P, VB, PITCH], BF16, name="embed_ones")
        src_sb = held.tile([E, N], BF16, name="src_sb")
        rel_sb = [held.tile([P, S], F32, name=f"rel{b}") for b in range(VB)]
        for b in range(HB):
            nc.sync.dma_start(embed_ones[:, b, 0:E], embed[b * P : (b + 1) * P, :])
        nc.sync.dma_start(src_sb[:], src_embed)
        nc.sync.dma_start(rel_sb[0][:], rel[0:P, :])
        for b in range(HB, VB):
            nc.sync.dma_start(embed_ones[:, b, 0:E], embed[b * P : (b + 1) * P, :])
        for b in range(1, VB):
            nc.sync.dma_start(rel_sb[b][:], rel[b * P : (b + 1) * P, :])
        nc.gpsimd.memset(embed_ones[:, :, E:W], 1.0)

        warm = held.tile([P, 2], F32, name="warm")
        nc.vector.memset(warm[:, 0:1], 1.0)
        nc.scalar.activation(warm[:, 1:2], warm[:, 0:1], ACT.Exp)

        ones = held.tile([P, N], BF16, name="ones")
        nc.gpsimd.memset(ones[:], 1.0)
        ident = held.tile([P, P], BF16, name="ident")
        make_identity(nc, ident[:])
        ident_f32 = held.tile([P, P], F32, name="ident_f32")
        make_identity(nc, ident_f32[:])

        expo = {}
        looked_up = {}
        gain = held.tile([P, VB, N], BF16, name="gain")
        picked = held.tile([P, VB, N], BF16, name="picked")
        finished = []
        mask_of = {}
        sums = {}

        def start_block(b):
            base_ps = setup_ps.tile([P, N], F32, name="base_ps", tag="setup")
            nc.tensor.matmul(base_ps[:], embT[:, b * P : (b + 1) * P], src_sb[:], start=True, stop=True)
            looked_up[b] = work.tile([P, N], F32, name="looked_up")
            nc.scalar.activation(looked_up[b][:], rel_sb[b][:].indirect(offsets[:]), ACT.Copy)
            expo[b] = work.tile([P, N], F32, name="expo")
            nc.scalar.activation(expo[b][:], base_ps[:], ACT.Exp)


        embT = held.tile([E, V], BF16, name="embT")
        for h in range(2):
            embT_ps = sums_ps.tile([E, HB * P], BF16, name="embT_ps", tag="bank")
            for i in range(HB):
                nc.tensor.transpose(embT_ps[:, i * P : (i + 1) * P], embed_ones[:, HB * h + i, 0:E], ident[:])
            nc.vector.tensor_copy(embT[:, HB * h * P : HB * (h + 1) * P], embT_ps[:])
            if h == 0:
                for b in range(AHEAD):
                    start_block(b)

        colsum_ps = sums_ps.tile([P, W], F32, name="colsum_ps", tag="bank")
        for b in range(VB):
            nc.tensor.matmul(colsum_ps[:], ones[:, 0:P], embed_ones[:, b, 0:W], start=(b == 0), stop=(b == VB - 1))
        rounded = held.tile([P, W], BF16, name="rounded")
        nc.vector.tensor_copy(rounded[:], colsum_ps[:])
        rest = held.tile([P, W], BF16, name="rest")
        nc.vector.tensor_sub(rest[:], colsum_ps[:], rounded[:])
        H = P // 2
        opening = held.tile([P, 2, W], BF16, name="opening")
        for i in range(2):
            nc.vector.tensor_scalar_mul(opening[0:H, i, :], rounded[0:H, :], 1.0 / H)
            nc.vector.tensor_scalar_mul(opening[H:P, i, :], rest[H:P, :], 1.0 / H)

        def open_banks(r):
            sums[r] = []
            for h in range(JC // 2):
                bank = sums_ps.tile([P, 2, W], F32, name="bank", tag="bank")
                nc.tensor.matmul(bank[:], ones[:, 0:P], opening[:], start=True, stop=False)
                sums[r].append(bank)

        def finish_block(b):
            if b + AHEAD < VB:
                start_block(b + AHEAD)
            nc.vector.tensor_copy(picked[:, b, :], looked_up[b][:])
            nc.vector.tensor_scalar(gain[:, b, :], expo[b][:], -1.0, 3.0e38, op0=ALU.add, op1=ALU.min)
            finished.append(b)


        def make_masks(r0, nr, b0, nb):
            for b in range(b0, b0 + nb):
                if b not in finished:
                    finish_block(b)
            mask = maskpool.tile([P, TILES, N], BF16, name="mask")
            for i in range(nr):
                nc.vector.tensor_single_scalar(
                    mask[:, i * nb : (i + 1) * nb, :], picked[:, b0 : b0 + nb, :], float(r0 + i + 1), op=ALU.is_equal
                )
            mask_of[r0, b0] = mask

        def add_step(r0, nr, b0, nb):
            q = qpool.tile([P, TILES, N], BF16, name="q")
            factor = gain[:, b0 : b0 + nb, :]
            if nr > 1:
                factor = factor.to_broadcast([P, nr, N])
            nc.vector.tensor_mul(q[:, 0 : nr * nb, :], mask_of[r0, b0][:, 0 : nr * nb, :], factor)
            for i in range(nr):
                for k in range(nb):
                    for c in range(JC):
                        nc.tensor.matmul(
                            sums[r0 + i][c // 2][:, c % 2, :],
                            q[:, i * nb + k, c * P : (c + 1) * P],
                            embed_ones[:, b0 + k, 0:W],
                            start=False,
                            stop=(b0 + k == VB - 1 and c % 2 == 1),
                        )

        def divide(r):
            quot = work.tile([P, JC, E], F32, name="quot")
            for h in range(JC // 2):
                recip = work.tile([P, 2, 1], F32, name="recip")
                if r == R - 1 and h == 1:
                    nc.vector.reciprocal(recip[:], sums[r][h][:, :, E : E + 1])
                    for i in range(2):
                        nc.vector.tensor_scalar_mul(quot[:, 2 * h + i, :], sums[r][h][:, i, 0:E], recip[:, i, :])
                else:
                    rsqrt = work.tile([P, 2, 1], F32, name="rsqrt")
                    nc.scalar.activation(rsqrt[:], sums[r][h][:, :, E : E + 1], ACT.Abs_reciprocal_sqrt)
                    nc.scalar.activation(recip[:], rsqrt[:], ACT.Square)
                    for i in range(2):
                        nc.scalar.activation(
                            quot[:, 2 * h + i, :], sums[r][h][:, i, 0:E], ACT.Identity, scale=recip[:, i, :]
                        )
            return quot

        def turn_back(r, quot):
            out_ps = setup_ps.tile([E, N], F32, name="out_ps", tag="setup")
            for c in range(JC):
                nc.tensor.transpose(out_ps[:, c * P : (c + 1) * P], quot[:, c, :], ident_f32[:])
            res = work.tile([E, N], F32, name="res")
            nc.scalar.copy(res[:], out_ps[:])
            nc.sync.dma_start(out[r * E : (r + 1) * E, :], res[:])

        steps = [(0, FIRST, b, 1) for b in range(VB)]
        steps += [(r, 1, b0, GROUP) for r in range(FIRST, R) for b0 in range(0, VB, GROUP)]
        divided = []
        make_masks(*steps[0])
        for s, (r0, nr, b0, nb) in enumerate(steps):
            if s + 1 < len(steps):
                make_masks(*steps[s + 1])
            if b0 == 0:
                for r in range(r0, r0 + nr):
                    open_banks(r)
            add_step(r0, nr, b0, nb)
            if r0 >= FIRST and s % 2 == 1 and divided:
                turn_back(*divided.pop(0))
            if b0 + nb == VB:
                for r in range(r0, r0 + nr):
                    divided.append((r, divide(r)))
        for r, quot in divided:
            turn_back(r, quot)
